import numpy as np
import ml_dtypes


def mxq(x, axis, fmt="e4m3"):
    dtype, down = {"e4m3": (ml_dtypes.float8_e4m3fn, 7), "e5m2": (ml_dtypes.float8_e5m2, 14)}[fmt]
    v = np.moveaxis(np.asarray(x, np.float32).astype(ml_dtypes.bfloat16).astype(np.float64), axis, -1)
    blocks = v.reshape(v.shape[:-1] + (-1, 32))
    amax = np.abs(blocks).max(-1, keepdims=True)
    byte = np.maximum(np.where(amax > 0, np.frexp(amax)[1] - 1 + 127, 0) - down, 1)
    scale = np.exp2(byte - 127.0)
    codes = (blocks / scale).astype(np.float32).astype(dtype).astype(np.float64)
    return np.moveaxis((codes * scale).reshape(v.shape), -1, axis)


WIDE = False


def mx_kscale(k):
    if not WIDE:
        return np.ones(k)
    levels = np.array([10, -10, 5, -5, 0])
    a = np.random.permutation(np.resize(levels, k // 512 * 4)).reshape(k // 512, 4)
    idx = np.arange(k)
    return np.exp2(a[idx // 512, idx % 128 // 32])


BF16 = ml_dtypes.bfloat16


def bf(x):
    return np.asarray(x, np.float32).astype(BF16)


def f64(x):
    return np.asarray(x).astype(np.float64)


E2M1 = np.array([0.0, 0.5, 1.0, 1.5, 2.0, 3.0, 4.0, 6.0, -0.0, -0.5, -1.0, -1.5, -2.0, -3.0, -4.0, -6.0])


def pack_weight(w, fmt):
    k, n = w.shape
    w = f64(bf(w)).reshape(k // 32, 32, n)
    amax = np.abs(w).max(1)
    if fmt == "e4m3":
        byte = np.frexp(amax)[1] - 1 + 127 - 7
    else:
        mant, ex = np.frexp(amax / 6.0)
        byte = np.where(mant > 0.5, ex, ex - 1) + 127
    byte = np.clip(np.where(amax > 0, byte, 1), 1, 254)
    scaled = (w * np.exp2(127.0 - byte)[:, None, :]).reshape(k, n).astype(np.float32)
    by_word = np.ascontiguousarray(scaled.reshape(k // 512, 128, 4, n).transpose(0, 1, 3, 2))
    if fmt == "e4m3":
        words = by_word.astype(ml_dtypes.float8_e4m3fn).view(np.uint8)
    else:
        c = by_word.astype(ml_dtypes.float4_e2m1fn).view(np.uint8) & 0xF
        words = c[..., 0::2] | (c[..., 1::2] << 4)
    return np.ascontiguousarray(words), np.ascontiguousarray(byte.astype(np.uint8).reshape(k // 512, 16, n))


def unpack_weight(words, scales, fmt):
    g, p, n, _ = words.shape
    if fmt == "e4m3":
        vals = np.ascontiguousarray(words).view(ml_dtypes.float8_e4m3fn).astype(np.float64)
    else:
        nib = np.empty((g, p, n, 4), np.uint8)
        nib[..., 0::2] = words & 0xF
        nib[..., 1::2] = words >> 4
        vals = E2M1[nib]
    vals = vals * np.repeat(np.exp2(scales.astype(np.float64) - 127.0), 8, axis=1)[..., None]
    return vals.transpose(0, 1, 3, 2).reshape(g * 512, n)

def pack4(w):
    words, scales = pack_weight(w, "e2m1")
    return words.reshape(words.shape[0], 128, -1), scales


def unpack4(words, scales):
    return unpack_weight(words.reshape(words.shape[0], 128, -1, 2), scales, "e2m1")


B, S, H, NH, FF = 2, 512, 1024, 8, 3072
EPS = 1e-7


def layer_norm(x, g, b):
    m = x.mean(-1, keepdims=True)
    v = ((x - m) ** 2).mean(-1, keepdims=True)
    return (x - m) / np.sqrt(v + EPS) * g + b


def setup_inputs():
    s = mx_kscale(FF)
    r = np.random.standard_normal
    ff = bf(r((B, S, FF)) * 0.65 * s)
    attn_out = bf(r((B, S, H)))
    Wf_words, Wf_scales = pack4(r((FF, H)) * 1.5 / np.sqrt(FF) / s[:, None])
    return {"ff": ff, "attn_out": attn_out,
            "Wf_words": Wf_words, "Wf_scales": Wf_scales, "b_f": bf(r(H) * 0.2),
            "ln2_g": bf(1.0 + 0.1 * r(H)), "ln2_b": bf(0.1 * r(H))}


def reference(ff, attn_out, Wf_words, Wf_scales, b_f, ln2_g, ln2_b):
    u = (mxq(f64(ff), 2, "e4m3") @ unpack4(Wf_words, Wf_scales)) + f64(b_f) + f64(attn_out)
    return layer_norm(u, f64(ln2_g), f64(ln2_b))

@@ -1,0 +1,220 @@
+from contextlib import ExitStack
+
+import concourse.mybir as mybir
+from concourse.masks import make_identity
+
+F32 = mybir.dt.float32
+BF16 = mybir.dt.bfloat16
+I32 = mybir.dt.int32
+U8 = mybir.dt.uint8
+U32 = mybir.dt.uint32
+FP8X4 = mybir.dt.float8_e4m3fn_x4
+FP4X4 = mybir.dt.float4_e2m1fn_x4
+ALU = mybir.AluOpType
+ACT = mybir.ActivationFunctionType
+
+P = 128
+TOKENS = 1024
+K = 3072
+N = 1024
+EPS = 1e-7
+K_PASS = 4 * P
+PASSES = K // K_PASS
+PAIRS_PER_PASS = K_PASS // 2
+TOKEN_TILES = TOKENS // P
+BANK = 512
+HALVES = N // BANK
+PASSES_PER_BANK = 2
+AHEAD = 2
+
+FLOPS = 2 * TOKENS * K * N
+
+
+def tile_disentangledattention_pc_kernel(
+    tc, ff, attn_out, Wf_words, Wf_scales, b_f, ln2_g, ln2_b, out
+):
+    nc = tc.nc
+    ff_rows = ff.rearrange("b s k -> (b s) k")
+    resid_rows = attn_out.rearrange("b s n -> (b s) n")
+    out_rows = out.rearrange("b s n -> (b s) n")
+
+    with ExitStack() as ctx:
+        consts = ctx.enter_context(tc.tile_pool(name="consts", bufs=1))
+        inputs = ctx.enter_context(tc.tile_pool(name="inputs", bufs=TOKEN_TILES))
+        grouped_pool = ctx.enter_context(tc.tile_pool(name="grouped", bufs=6))
+        codes_pool = ctx.enter_context(tc.tile_pool(name="codes", bufs=AHEAD + 1))
+        rows_pool = ctx.enter_context(tc.tile_pool(name="rows", bufs=3))
+        stats = ctx.enter_context(tc.tile_pool(name="stats", bufs=3))
+        flipped_pool = ctx.enter_context(tc.psum_pool(name="flipped", bufs=4))
+        acc_pool = ctx.enter_context(tc.psum_pool(name="acc", bufs=4))
+        ctx.enter_context(tc.manual_schedule())
+
+        w_words = consts.tile([P, PASSES, 2 * N], U8, align_bytes=64)
+        w_planes = consts.tile([P, PASSES, N], U8, align_bytes=64)
+        vec_rows = consts.tile([P, 3, N], BF16)
+        ones = consts.tile([P, P], BF16)
+        ident = consts.tile([P, P], F32)
+        eps = consts.tile([P, 1], F32)
+        warm = consts.tile([P, 1], F32)
+        nc.vector.memset(w_planes[:].bitcast(I32), 0)
+        nc.vector.memset(vec_rows[:].bitcast(I32), 0)
+        nc.vector.memset(ones[:], 1.0)
+        nc.vector.memset(eps[:], EPS)
+        make_identity(nc, ident[:])
+        nc.scalar.activation(out=warm[:], in_=eps[:], func=ACT.Sqrt)
+
+        ff_tiles = []
+        resid_tiles = []
+
+        def load_ff(i):
+            ff_sb = inputs.tile([P, K], BF16)
+            nc.sync.dma_start(out=ff_sb[:], in_=ff_rows[P * i : P * (i + 1), :])
+            ff_tiles.append(ff_sb)
+
+        def load_resid(i):
+            resid_sb = inputs.tile([P, N], BF16)
+            nc.sync.dma_start(out=resid_sb[:], in_=resid_rows[P * i : P * (i + 1), :])
+            resid_tiles.append(resid_sb)
+
+        for i in range(AHEAD):
+            load_ff(i)
+        for j, vec in enumerate((b_f, ln2_g, ln2_b)):
+            nc.scalar.dma_start(out=vec_rows[0:1, j, :], in_=vec.unsqueeze(0))
+        scale_rows = Wf_scales.bitcast(I32).rearrange("g (j b r) n -> b r j g n", j=2, b=2, r=4)
+        planes_i32 = w_planes[:].bitcast(I32)
+        for b in range(2):
+            for r in range(4):
+                nc.sync.dma_start(out=planes_i32[32 * b + r : P : 64], in_=scale_rows[b, r])
+        for g in range(PASSES):
+            nc.sync.dma_start(out=w_words[:, g, :].bitcast(I32), in_=Wf_words[g].bitcast(I32))
+        for i in range(TOKEN_TILES):
+            if i + AHEAD < TOKEN_TILES:
+                load_ff(i + AHEAD)
+            load_resid(i)
+
+        grouped_tiles = {}
+        code_tiles = {}
+
+        def transpose(i):
+            pairs = ff_tiles[i][:].bitcast(F32)
+            for bank in range(PASSES // PASSES_PER_BANK):
+                flipped = flipped_pool.tile([P, PASSES_PER_BANK, 2, P], F32)
+                for gg in range(PASSES_PER_BANK):
+                    first = PAIRS_PER_PASS * (PASSES_PER_BANK * bank + gg)
+                    for u in range(2):
+                        nc.tensor.transpose(
+                            flipped[:, gg, u, :],
+                            pairs[:, first + u : first + PAIRS_PER_PASS : 2],
+                            ident[:],
+                        )
+                grouped = grouped_pool.tile([P, PASSES_PER_BANK, P, 4], BF16, align_bytes=64)
+                nc.scalar.copy(
+                    out=grouped[:].bitcast(F32), in_=flipped[:].rearrange("p g u t -> p g t u")
+                )
+                grouped_tiles[(i, bank)] = grouped
+
+        def quantise(i):
+            codes = codes_pool.tile([P, PASSES, P], U32, align_bytes=64)
+            planes = codes_pool.tile([P, PASSES, P], U8, align_bytes=64)
+            for bank in range(PASSES // PASSES_PER_BANK):
+                some = slice(PASSES_PER_BANK * bank, PASSES_PER_BANK * (bank + 1))
+                nc.vector.quantize_mx(
+                    out=codes[:, some, :].rearrange("p g t -> p (g t)").bitcast(FP8X4),
+                    scales=planes[:, some, :].rearrange("p g t -> p (g t)"),
+                    in_=grouped_tiles[(i, bank)][:].rearrange("p g t e -> p (g t e)"),
+                )
+            code_tiles[i] = (codes, planes)
+
+        def multiply(i):
+            codes, planes = code_tiles[i]
+            accs = [acc_pool.tile([P, BANK], F32, name="acc") for h in range(HALVES)]
+            for g in range(PASSES):
+                for h in range(HALVES):
+                    nc.tensor.matmul_mx(
+                        out=accs[h][:],
+                        lhsT=codes[:, g, :].bitcast(FP8X4),
+                        lhsT_scale=planes[:, g, :],
+                        rhs=w_words[:, g, 2 * BANK * h : 2 * BANK * (h + 1)].bitcast(FP4X4),
+                        rhs_scale=w_planes[:, g, BANK * h : BANK * (h + 1)],
+                        start=(g == 0),
+                        stop=(g == PASSES - 1),
+                    )
+            return accs
+
+        biased_tiles = {}
+
+        def add_bias(i):
+            biased = inputs.tile([P, N], F32)
+            nc.vector.tensor_tensor(out=biased[:], in0=resid_tiles[i][:], in1=spread[0][:], op=ALU.add)
+            biased_tiles[i] = biased
+
+        for i in range(AHEAD):
+            transpose(i)
+            quantise(i)
+        spread = []
+        for j in range(3):
+            wide = consts.tile([P, N], F32, name="wide%d" % j)
+            for h in range(HALVES):
+                cols = slice(BANK * h, BANK * (h + 1))
+                acc = acc_pool.tile([P, BANK], F32, name="acc")
+                nc.tensor.matmul(acc[:], lhsT=ones[:], rhs=vec_rows[:, j, cols], start=True, stop=True)
+                nc.vector.tensor_copy(out=wide[:, cols], in_=acc[:])
+            spread.append(wide)
+        gain = spread[1]
+        shift = spread[2]
+        add_bias(0)
+
+        for i in range(TOKEN_TILES):
+            accs = multiply(i)
+
+            u = rows_pool.tile([P, N], F32)
+            sums = stats.tile([P, HALVES], F32)
+            negmean = stats.tile([P, 1], F32)
+            for h in range(HALVES):
+                cols = slice(BANK * h, BANK * (h + 1))
+                nc.vector.scalar_tensor_tensor(
+                    out=u[:, cols],
+                    in0=accs[h][:],
+                    scalar=1.0,
+                    in1=biased_tiles[i][:, cols],
+                    op0=ALU.mult,
+                    op1=ALU.add,
+                    accum_out=sums[:, h : h + 1],
+                )
+            nc.vector.tensor_scalar(
+                out=negmean[:],
+                in0=sums[:, 0:1],
+                scalar1=sums[:, 1:2],
+                scalar2=-1.0 / N,
+                op0=ALU.add,
+                op1=ALU.mult,
+            )
+
+            if i + AHEAD < TOKEN_TILES:
+                transpose(i + AHEAD)
+
+            squares = rows_pool.tile([P, N], BF16)
+            sumsq = stats.tile([P, 1], F32)
+            std = stats.tile([P, 1], F32)
+            nc.scalar.activation(
+                out=squares[:], in_=u[:], func=ACT.Square, bias=negmean[:], scale=1.0, accum_out=sumsq[:]
+            )
+            nc.scalar.activation(out=std[:], in_=sumsq[:], func=ACT.Sqrt, bias=eps[:], scale=1.0 / N)
+
+            y = rows_pool.tile([P, N], F32)
+            nc.vector.scalar_tensor_tensor(
+                out=y[:], in0=u[:], scalar=negmean[:], in1=gain[:], op0=ALU.add, op1=ALU.mult
+            )
+
+            if i + AHEAD < TOKEN_TILES:
+                quantise(i + AHEAD)
+
+            rstd = stats.tile([P, 1], F32)
+            nc.vector.reciprocal(out=rstd[:], in_=std[:])
+            nc.vector.scalar_tensor_tensor(
+                out=y[:], in0=y[:], scalar=rstd[:], in1=shift[:], op0=ALU.mult, op1=ALU.add
+            )
+            nc.sync.dma_start(out=out_rows[P * i : P * (i + 1), :], in_=y[:])
+
+            if i + 1 < TOKEN_TILES:
+                add_bias(i + 1)

@@ -45,8 +45,9 @@ def tile_disentangledattention_pc_kernel(
         codes_pool = ctx.enter_context(tc.tile_pool(name="codes", bufs=AHEAD + 1))
         rows_pool = ctx.enter_context(tc.tile_pool(name="rows", bufs=3))
         stats = ctx.enter_context(tc.tile_pool(name="stats", bufs=3))
-        flipped_pool = ctx.enter_context(tc.psum_pool(name="flipped", bufs=4))
-        acc_pool = ctx.enter_context(tc.psum_pool(name="acc", bufs=4))
+        spread_pool = ctx.enter_context(tc.psum_pool(name="spread", bufs=1))
+        flipped_pool = ctx.enter_context(tc.psum_pool(name="flipped", bufs=3))
+        acc_pool = ctx.enter_context(tc.psum_pool(name="acc", bufs=3))
         ctx.enter_context(tc.manual_schedule())
 
         w_words = consts.tile([P, PASSES, 2 * N], U8, align_bytes=64)
@@ -78,6 +79,7 @@ def tile_disentangledattention_pc_kernel(
 
         for i in range(AHEAD):
             load_ff(i)
+        load_resid(0)
         for j, vec in enumerate((b_f, ln2_g, ln2_b)):
             nc.scalar.dma_start(out=vec_rows[0:1, j, :], in_=vec.unsqueeze(0))
         scale_rows = Wf_scales.bitcast(I32).rearrange("g (j b r) n -> b r j g n", j=2, b=2, r=4)
@@ -90,7 +92,8 @@ def tile_disentangledattention_pc_kernel(
         for i in range(TOKEN_TILES):
             if i + AHEAD < TOKEN_TILES:
                 load_ff(i + AHEAD)
-            load_resid(i)
+            if i + 1 < TOKEN_TILES:
+                load_resid(i + 1)
 
         grouped_tiles = {}
         code_tiles = {}
@@ -145,24 +148,30 @@ def tile_disentangledattention_pc_kernel(
 
         def add_bias(i):
             biased = inputs.tile([P, N], F32)
-            nc.vector.tensor_tensor(out=biased[:], in0=resid_tiles[i][:], in1=spread[0][:], op=ALU.add)
+            for h in range(HALVES):
+                cols = slice(BANK * h, BANK * (h + 1))
+                nc.gpsimd.tensor_tensor(
+                    out=biased[:, cols], in0=resid_tiles[i][:, cols], in1=bias[:, cols], op=ALU.add
+                )
             biased_tiles[i] = biased
 
         for i in range(AHEAD):
             transpose(i)
             quantise(i)
-        spread = []
-        for j in range(3):
-            wide = consts.tile([P, N], F32, name="wide%d" % j)
-            for h in range(HALVES):
-                cols = slice(BANK * h, BANK * (h + 1))
-                acc = acc_pool.tile([P, BANK], F32, name="acc")
-                nc.tensor.matmul(acc[:], lhsT=ones[:], rhs=vec_rows[:, j, cols], start=True, stop=True)
-                nc.vector.tensor_copy(out=wide[:, cols], in_=acc[:])
-            spread.append(wide)
-        gain = spread[1]
-        shift = spread[2]
-        add_bias(0)
+        bias = consts.tile([P, N], BF16)
+        gain = spread_pool.tile([P, N], BF16)
+        shift = spread_pool.tile([P, N], BF16)
+        for h in range(HALVES):
+            cols = slice(BANK * h, BANK * (h + 1))
+            acc = acc_pool.tile([P, BANK], F32, name="acc")
+            nc.tensor.matmul(acc[:], lhsT=ones[:], rhs=vec_rows[:, 0, cols], start=True, stop=True)
+            nc.vector.tensor_copy(out=bias[:, cols], in_=acc[:])
+        for h in range(HALVES):
+            cols = slice(BANK * h, BANK * (h + 1))
+            nc.tensor.matmul(gain[:, cols], lhsT=ones[:], rhs=vec_rows[:, 1, cols], start=True, stop=True)
+            nc.tensor.matmul(shift[:, cols], lhsT=ones[:], rhs=vec_rows[:, 2, cols], start=True, stop=True)
+        for i in range(TOKEN_TILES):
+            add_bias(i)
 
         for i in range(TOKEN_TILES):
             accs = multiply(i)
@@ -215,6 +224,3 @@ def tile_disentangledattention_pc_kernel(
                 out=y[:], in0=y[:], scalar=rstd[:], in1=shift[:], op0=ALU.mult, op1=ALU.add
             )
             nc.sync.dma_start(out=out_rows[P * i : P * (i + 1), :], in_=y[:])
-
-            if i + 1 < TOKEN_TILES:
-                add_bias(i + 1)

@@ -87,8 +87,11 @@ def tile_disentangledattention_pc_kernel(
         for b in range(2):
             for r in range(4):
                 nc.sync.dma_start(out=planes_i32[32 * b + r : P : 64], in_=scale_rows[b, r])
-        for g in range(PASSES):
-            nc.sync.dma_start(out=w_words[:, g, :].bitcast(I32), in_=Wf_words[g].bitcast(I32))
+        word_rows = Wf_words.bitcast(I32).rearrange("g p (h c) -> h p g c", h=HALVES)
+        words_i32 = w_words[:].bitcast(I32).rearrange("p g (h c) -> h p g c", h=HALVES)
+        for h in range(HALVES):
+            for g in range(0, PASSES, 2):
+                nc.sync.dma_start(out=words_i32[h][:, g : g + 2, :], in_=word_rows[h][:, g : g + 2, :])
         for i in range(TOKEN_TILES):
             if i + AHEAD < TOKEN_TILES:
                 load_ff(i + AHEAD)
@@ -131,8 +134,8 @@ def tile_disentangledattention_pc_kernel(
         def multiply(i):
             codes, planes = code_tiles[i]
             accs = [acc_pool.tile([P, BANK], F32, name="acc") for h in range(HALVES)]
-            for g in range(PASSES):
-                for h in range(HALVES):
+            for h in range(HALVES):
+                for g in range(PASSES):
                     nc.tensor.matmul_mx(
                         out=accs[h][:],
                         lhsT=codes[:, g, :].bitcast(FP8X4),
@@ -173,6 +176,18 @@ def tile_disentangledattention_pc_kernel(
         for i in range(TOKEN_TILES):
             add_bias(i)
 
+        y_tiles = {}
+        std_tiles = {}
+
+        def finish(i):
+            rstd = stats.tile([P, 1], F32)
+            y = y_tiles[i]
+            nc.vector.reciprocal(out=rstd[:], in_=std_tiles[i][:])
+            nc.vector.scalar_tensor_tensor(
+                out=y[:], in0=y[:], scalar=rstd[:], in1=shift[:], op0=ALU.mult, op1=ALU.add
+            )
+            nc.sync.dma_start(out=out_rows[P * i : P * (i + 1), :], in_=y[:])
+
         for i in range(TOKEN_TILES):
             accs = multiply(i)
 
@@ -198,6 +213,8 @@ def tile_disentangledattention_pc_kernel(
                 op0=ALU.add,
                 op1=ALU.mult,
             )
+            if i > 0:
+                finish(i - 1)
 
             if i + AHEAD < TOKEN_TILES:
                 transpose(i + AHEAD)
@@ -209,18 +226,14 @@ def tile_disentangledattention_pc_kernel(
                 out=squares[:], in_=u[:], func=ACT.Square, bias=negmean[:], scale=1.0, accum_out=sumsq[:]
             )
             nc.scalar.activation(out=std[:], in_=sumsq[:], func=ACT.Sqrt, bias=eps[:], scale=1.0 / N)
+            std_tiles[i] = std
 
             y = rows_pool.tile([P, N], F32)
             nc.vector.scalar_tensor_tensor(
                 out=y[:], in0=u[:], scalar=negmean[:], in1=gain[:], op0=ALU.add, op1=ALU.mult
             )
+            y_tiles[i] = y
 
             if i + AHEAD < TOKEN_TILES:
                 quantise(i + AHEAD)
-
-            rstd = stats.tile([P, 1], F32)
-            nc.vector.reciprocal(out=rstd[:], in_=std[:])
-            nc.vector.scalar_tensor_tensor(
-                out=y[:], in0=y[:], scalar=rstd[:], in1=shift[:], op0=ALU.mult, op1=ALU.add
-            )
-            nc.sync.dma_start(out=out_rows[P * i : P * (i + 1), :], in_=y[:])
+        finish(TOKEN_TILES - 1)

@@ -25,7 +25,9 @@ TOKEN_TILES = TOKENS // P
 BANK = 512
 HALVES = N // BANK
 PASSES_PER_BANK = 2
+FLIP_BANKS = PASSES // PASSES_PER_BANK
 AHEAD = 2
+ROW_BUFS = 3
 
 FLOPS = 2 * TOKENS * K * N
 
@@ -37,16 +39,17 @@ def tile_disentangledattention_pc_kernel(
     ff_rows = ff.rearrange("b s k -> (b s) k")
     resid_rows = attn_out.rearrange("b s n -> (b s) n")
     out_rows = out.rearrange("b s n -> (b s) n")
+    halves = [slice(BANK * h, BANK * (h + 1)) for h in range(HALVES)]
 
     with ExitStack() as ctx:
         consts = ctx.enter_context(tc.tile_pool(name="consts", bufs=1))
         inputs = ctx.enter_context(tc.tile_pool(name="inputs", bufs=TOKEN_TILES))
-        grouped_pool = ctx.enter_context(tc.tile_pool(name="grouped", bufs=6))
-        codes_pool = ctx.enter_context(tc.tile_pool(name="codes", bufs=AHEAD + 1))
-        rows_pool = ctx.enter_context(tc.tile_pool(name="rows", bufs=3))
-        stats = ctx.enter_context(tc.tile_pool(name="stats", bufs=3))
+        grouped_pool = ctx.enter_context(tc.tile_pool(name="grouped", bufs=2 * FLIP_BANKS))
+        codes_pool = ctx.enter_context(tc.tile_pool(name="codes", bufs=2))
+        rows_pool = ctx.enter_context(tc.tile_pool(name="rows", bufs=ROW_BUFS))
+        stats = ctx.enter_context(tc.tile_pool(name="stats", bufs=ROW_BUFS))
         spread_pool = ctx.enter_context(tc.psum_pool(name="spread", bufs=1))
-        flipped_pool = ctx.enter_context(tc.psum_pool(name="flipped", bufs=3))
+        flipped_pool = ctx.enter_context(tc.psum_pool(name="flipped", bufs=FLIP_BANKS))
         acc_pool = ctx.enter_context(tc.psum_pool(name="acc", bufs=3))
         ctx.enter_context(tc.manual_schedule())
 
@@ -57,8 +60,8 @@ def tile_disentangledattention_pc_kernel(
         ident = consts.tile([P, P], F32)
         eps = consts.tile([P, 1], F32)
         warm = consts.tile([P, 1], F32)
-        nc.vector.memset(w_planes[:].bitcast(I32), 0)
         nc.vector.memset(vec_rows[:].bitcast(I32), 0)
+        nc.vector.memset(w_planes[:].bitcast(I32), 0)
         nc.vector.memset(ones[:], 1.0)
         nc.vector.memset(eps[:], EPS)
         make_identity(nc, ident[:])
@@ -77,33 +80,33 @@ def tile_disentangledattention_pc_kernel(
             nc.sync.dma_start(out=resid_sb[:], in_=resid_rows[P * i : P * (i + 1), :])
             resid_tiles.append(resid_sb)
 
-        for i in range(AHEAD):
-            load_ff(i)
-        load_resid(0)
         for j, vec in enumerate((b_f, ln2_g, ln2_b)):
-            nc.scalar.dma_start(out=vec_rows[0:1, j, :], in_=vec.unsqueeze(0))
-        scale_rows = Wf_scales.bitcast(I32).rearrange("g (j b r) n -> b r j g n", j=2, b=2, r=4)
+            nc.gpsimd.dma_start(out=vec_rows[0:1, j, :], in_=vec.unsqueeze(0))
+        load_ff(0)
+        scale_rows = Wf_scales.bitcast(I32).rearrange("g (q r) n -> r q g n", r=4)
         planes_i32 = w_planes[:].bitcast(I32)
-        for b in range(2):
-            for r in range(4):
-                nc.sync.dma_start(out=planes_i32[32 * b + r : P : 64], in_=scale_rows[b, r])
+        for r in range(4):
+            nc.sync.dma_start(out=planes_i32[r : P : 32], in_=scale_rows[r])
+        load_ff(1)
+        load_resid(0)
         word_rows = Wf_words.bitcast(I32).rearrange("g p (h c) -> h p g c", h=HALVES)
         words_i32 = w_words[:].bitcast(I32).rearrange("p g (h c) -> h p g c", h=HALVES)
         for h in range(HALVES):
-            for g in range(0, PASSES, 2):
-                nc.sync.dma_start(out=words_i32[h][:, g : g + 2, :], in_=word_rows[h][:, g : g + 2, :])
-        for i in range(TOKEN_TILES):
-            if i + AHEAD < TOKEN_TILES:
-                load_ff(i + AHEAD)
-            if i + 1 < TOKEN_TILES:
-                load_resid(i + 1)
+            for g in range(0, PASSES, 3):
+                nc.sync.dma_start(out=words_i32[h][:, g : g + 3, :], in_=word_rows[h][:, g : g + 3, :])
+        for i in range(AHEAD, TOKEN_TILES + 1):
+            if i < TOKEN_TILES:
+                load_ff(i)
+            load_resid(i - 1)
 
+        flipped_tiles = {}
         grouped_tiles = {}
         code_tiles = {}
+        biased_tiles = {}
 
         def transpose(i):
             pairs = ff_tiles[i][:].bitcast(F32)
-            for bank in range(PASSES // PASSES_PER_BANK):
+            for bank in range(FLIP_BANKS):
                 flipped = flipped_pool.tile([P, PASSES_PER_BANK, 2, P], F32)
                 for gg in range(PASSES_PER_BANK):
                     first = PAIRS_PER_PASS * (PASSES_PER_BANK * bank + gg)
@@ -113,6 +116,11 @@ def tile_disentangledattention_pc_kernel(
                             pairs[:, first + u : first + PAIRS_PER_PASS : 2],
                             ident[:],
                         )
+                flipped_tiles[(i, bank)] = flipped
+
+        def regroup(i):
+            for bank in range(FLIP_BANKS):
+                flipped = flipped_tiles[(i, bank)]
                 grouped = grouped_pool.tile([P, PASSES_PER_BANK, P, 4], BF16, align_bytes=64)
                 nc.scalar.copy(
                     out=grouped[:].bitcast(F32), in_=flipped[:].rearrange("p g u t -> p g t u")
@@ -122,7 +130,7 @@ def tile_disentangledattention_pc_kernel(
         def quantise(i):
             codes = codes_pool.tile([P, PASSES, P], U32, align_bytes=64)
             planes = codes_pool.tile([P, PASSES, P], U8, align_bytes=64)
-            for bank in range(PASSES // PASSES_PER_BANK):
+            for bank in range(FLIP_BANKS):
                 some = slice(PASSES_PER_BANK * bank, PASSES_PER_BANK * (bank + 1))
                 nc.vector.quantize_mx(
                     out=codes[:, some, :].rearrange("p g t -> p (g t)").bitcast(FP8X4),
@@ -141,70 +149,66 @@ def tile_disentangledattention_pc_kernel(
                         lhsT=codes[:, g, :].bitcast(FP8X4),
                         lhsT_scale=planes[:, g, :],
                         rhs=w_words[:, g, 2 * BANK * h : 2 * BANK * (h + 1)].bitcast(FP4X4),
-                        rhs_scale=w_planes[:, g, BANK * h : BANK * (h + 1)],
+                        rhs_scale=w_planes[:, g, halves[h]],
                         start=(g == 0),
                         stop=(g == PASSES - 1),
                     )
             return accs
 
-        biased_tiles = {}
-
         def add_bias(i):
-            biased = inputs.tile([P, N], F32)
-            for h in range(HALVES):
-                cols = slice(BANK * h, BANK * (h + 1))
+            biased = rows_pool.tile([P, N], F32)
+            for cols in halves:
                 nc.gpsimd.tensor_tensor(
                     out=biased[:, cols], in0=resid_tiles[i][:, cols], in1=bias[:, cols], op=ALU.add
                 )
             biased_tiles[i] = biased
 
-        for i in range(AHEAD):
-            transpose(i)
-            quantise(i)
-        bias = consts.tile([P, N], BF16)
-        gain = spread_pool.tile([P, N], BF16)
-        shift = spread_pool.tile([P, N], BF16)
-        for h in range(HALVES):
-            cols = slice(BANK * h, BANK * (h + 1))
-            acc = acc_pool.tile([P, BANK], F32, name="acc")
-            nc.tensor.matmul(acc[:], lhsT=ones[:], rhs=vec_rows[:, 0, cols], start=True, stop=True)
-            nc.vector.tensor_copy(out=bias[:, cols], in_=acc[:])
-        for h in range(HALVES):
-            cols = slice(BANK * h, BANK * (h + 1))
-            nc.tensor.matmul(gain[:, cols], lhsT=ones[:], rhs=vec_rows[:, 1, cols], start=True, stop=True)
-            nc.tensor.matmul(shift[:, cols], lhsT=ones[:], rhs=vec_rows[:, 2, cols], start=True, stop=True)
-        for i in range(TOKEN_TILES):
-            add_bias(i)
-
-        y_tiles = {}
-        std_tiles = {}
-
         def finish(i):
+            y, std = unfinished[i]
             rstd = stats.tile([P, 1], F32)
-            y = y_tiles[i]
-            nc.vector.reciprocal(out=rstd[:], in_=std_tiles[i][:])
+            nc.vector.reciprocal(out=rstd[:], in_=std[:])
             nc.vector.scalar_tensor_tensor(
                 out=y[:], in0=y[:], scalar=rstd[:], in1=shift[:], op0=ALU.mult, op1=ALU.add
             )
             nc.sync.dma_start(out=out_rows[P * i : P * (i + 1), :], in_=y[:])
 
-        for i in range(TOKEN_TILES):
-            accs = multiply(i)
+        transpose(0)
+        regroup(0)
+        quantise(0)
+        bias = consts.tile([P, N], BF16)
+        gain = spread_pool.tile([P, N], BF16)
+        shift = spread_pool.tile([P, N], BF16)
+        for cols in halves:
+            acc = acc_pool.tile([P, BANK], F32, name="acc")
+            nc.tensor.matmul(acc[:], lhsT=ones[:], rhs=vec_rows[:, 0, cols], start=True, stop=True)
+            nc.vector.tensor_copy(out=bias[:, cols], in_=acc[:])
+        for i in range(ROW_BUFS):
+            add_bias(i)
+        transpose(1)
+        regroup(1)
+        next_accs = multiply(0)
+        for cols in halves:
+            nc.tensor.matmul(gain[:, cols], lhsT=ones[:], rhs=vec_rows[:, 1, cols], start=True, stop=True)
+            nc.tensor.matmul(shift[:, cols], lhsT=ones[:], rhs=vec_rows[:, 2, cols], start=True, stop=True)
 
+        unfinished = {}
+        for i in range(TOKEN_TILES):
+            accs = next_accs
             u = rows_pool.tile([P, N], F32)
             sums = stats.tile([P, HALVES], F32)
             negmean = stats.tile([P, 1], F32)
             for h in range(HALVES):
-                cols = slice(BANK * h, BANK * (h + 1))
                 nc.vector.scalar_tensor_tensor(
-                    out=u[:, cols],
+                    out=u[:, halves[h]],
                     in0=accs[h][:],
                     scalar=1.0,
-                    in1=biased_tiles[i][:, cols],
+                    in1=biased_tiles[i][:, halves[h]],
                     op0=ALU.mult,
                     op1=ALU.add,
                     accum_out=sums[:, h : h + 1],
                 )
+                if h == 0 and i + 1 < TOKEN_TILES:
+                    quantise(i + 1)
             nc.vector.tensor_scalar(
                 out=negmean[:],
                 in0=sums[:, 0:1],
@@ -218,6 +222,8 @@ def tile_disentangledattention_pc_kernel(
 
             if i + AHEAD < TOKEN_TILES:
                 transpose(i + AHEAD)
+            if i + 1 < TOKEN_TILES:
+                next_accs = multiply(i + 1)
 
             squares = rows_pool.tile([P, N], BF16)
             sumsq = stats.tile([P, 1], F32)
@@ -226,14 +232,15 @@ def tile_disentangledattention_pc_kernel(
                 out=squares[:], in_=u[:], func=ACT.Square, bias=negmean[:], scale=1.0, accum_out=sumsq[:]
             )
             nc.scalar.activation(out=std[:], in_=sumsq[:], func=ACT.Sqrt, bias=eps[:], scale=1.0 / N)
-            std_tiles[i] = std
+            if i + AHEAD < TOKEN_TILES:
+                regroup(i + AHEAD)
 
             y = rows_pool.tile([P, N], F32)
             nc.vector.scalar_tensor_tensor(
                 out=y[:], in0=u[:], scalar=negmean[:], in1=gain[:], op0=ALU.add, op1=ALU.mult
             )
-            y_tiles[i] = y
+            unfinished[i] = (y, std)
 
-            if i + AHEAD < TOKEN_TILES:
-                quantise(i + AHEAD)
+            if i + ROW_BUFS < TOKEN_TILES:
+                add_bias(i + ROW_BUFS)
         finish(TOKEN_TILES - 1)

@@ -28,6 +28,8 @@ PASSES_PER_BANK = 2
 FLIP_BANKS = PASSES // PASSES_PER_BANK
 AHEAD = 2
 ROW_BUFS = 3
+FIRST_SORTED = 4
+SORT_AHEAD = 4
 
 FLOPS = 2 * TOKENS * K * N
 
@@ -44,6 +46,7 @@ def tile_disentangledattention_pc_kernel(
     with ExitStack() as ctx:
         consts = ctx.enter_context(tc.tile_pool(name="consts", bufs=1))
         inputs = ctx.enter_context(tc.tile_pool(name="inputs", bufs=TOKEN_TILES))
+        sorted_pool = ctx.enter_context(tc.tile_pool(name="sorted", bufs=3))
         grouped_pool = ctx.enter_context(tc.tile_pool(name="grouped", bufs=2 * FLIP_BANKS))
         codes_pool = ctx.enter_context(tc.tile_pool(name="codes", bufs=2))
         rows_pool = ctx.enter_context(tc.tile_pool(name="rows", bufs=ROW_BUFS))
@@ -65,7 +68,7 @@ def tile_disentangledattention_pc_kernel(
         nc.vector.memset(ones[:], 1.0)
         nc.vector.memset(eps[:], EPS)
         make_identity(nc, ident[:])
-        nc.scalar.activation(out=warm[:], in_=eps[:], func=ACT.Sqrt)
+        nc.scalar.activation(out=warm[:], in_=eps[:], func=ACT.Abs_reciprocal_sqrt)
 
         ff_tiles = []
         resid_tiles = []
@@ -104,6 +107,14 @@ def tile_disentangledattention_pc_kernel(
         code_tiles = {}
         biased_tiles = {}
 
+        sorted_tiles = {}
+
+        def sort_words(i):
+            pairs = ff_tiles[i][:].bitcast(F32)
+            in_order = sorted_pool.tile([P, PASSES, 2, P], F32)
+            nc.scalar.copy(out=in_order[:], in_=pairs.rearrange("t (g p u) -> t g u p", g=PASSES, u=2))
+            sorted_tiles[i] = in_order
+
         def transpose(i):
             pairs = ff_tiles[i][:].bitcast(F32)
             for bank in range(FLIP_BANKS):
@@ -111,11 +122,11 @@ def tile_disentangledattention_pc_kernel(
                 for gg in range(PASSES_PER_BANK):
                     first = PAIRS_PER_PASS * (PASSES_PER_BANK * bank + gg)
                     for u in range(2):
-                        nc.tensor.transpose(
-                            flipped[:, gg, u, :],
-                            pairs[:, first + u : first + PAIRS_PER_PASS : 2],
-                            ident[:],
-                        )
+                        if i in sorted_tiles:
+                            words = sorted_tiles[i][:, PASSES_PER_BANK * bank + gg, u, :]
+                        else:
+                            words = pairs[:, first + u : first + PAIRS_PER_PASS : 2]
+                        nc.tensor.transpose(flipped[:, gg, u, :], words, ident[:])
                 flipped_tiles[(i, bank)] = flipped
 
         def regroup(i):
@@ -164,9 +175,7 @@ def tile_disentangledattention_pc_kernel(
             biased_tiles[i] = biased
 
         def finish(i):
-            y, std = unfinished[i]
-            rstd = stats.tile([P, 1], F32)
-            nc.vector.reciprocal(out=rstd[:], in_=std[:])
+            y, rstd = unfinished[i]
             nc.vector.scalar_tensor_tensor(
                 out=y[:], in0=y[:], scalar=rstd[:], in1=shift[:], op0=ALU.mult, op1=ALU.add
             )
@@ -209,13 +218,9 @@ def tile_disentangledattention_pc_kernel(
                 )
                 if h == 0 and i + 1 < TOKEN_TILES:
                     quantise(i + 1)
-            nc.vector.tensor_scalar(
-                out=negmean[:],
-                in0=sums[:, 0:1],
-                scalar1=sums[:, 1:2],
-                scalar2=-1.0 / N,
-                op0=ALU.add,
-                op1=ALU.mult,
+            scaled = stats.tile([P, HALVES], F32)
+            nc.scalar.activation(
+                out=scaled[:], in_=sums[:], func=ACT.Copy, scale=-1.0 / N, accum_out=negmean[:]
             )
             if i > 0:
                 finish(i - 1)
@@ -227,19 +232,23 @@ def tile_disentangledattention_pc_kernel(
 
             squares = rows_pool.tile([P, N], BF16)
             sumsq = stats.tile([P, 1], F32)
-            std = stats.tile([P, 1], F32)
+            rstd = stats.tile([P, 1], F32)
             nc.scalar.activation(
                 out=squares[:], in_=u[:], func=ACT.Square, bias=negmean[:], scale=1.0, accum_out=sumsq[:]
             )
-            nc.scalar.activation(out=std[:], in_=sumsq[:], func=ACT.Sqrt, bias=eps[:], scale=1.0 / N)
+            nc.scalar.activation(
+                out=rstd[:], in_=sumsq[:], func=ACT.Abs_reciprocal_sqrt, bias=eps[:], scale=1.0 / N
+            )
             if i + AHEAD < TOKEN_TILES:
                 regroup(i + AHEAD)
+            if FIRST_SORTED <= i + SORT_AHEAD < TOKEN_TILES:
+                sort_words(i + SORT_AHEAD)
 
             y = rows_pool.tile([P, N], F32)
             nc.vector.scalar_tensor_tensor(
                 out=y[:], in0=u[:], scalar=negmean[:], in1=gain[:], op0=ALU.add, op1=ALU.mult
             )
-            unfinished[i] = (y, std)
+            unfinished[i] = (y, rstd)
 
             if i + ROW_BUFS < TOKEN_TILES:
                 add_bias(i + ROW_BUFS)

@@ -64,6 +64,8 @@ def tile_disentangledattention_pc_kernel(
         eps = consts.tile([P, 1], F32)
         warm = consts.tile([P, 1], F32)
         nc.vector.memset(vec_rows[:].bitcast(I32), 0)
+        for j, vec in enumerate((b_f, ln2_g, ln2_b)):
+            nc.scalar.dma_start(out=vec_rows[0:1, j, :], in_=vec.unsqueeze(0))
         nc.vector.memset(w_planes[:].bitcast(I32), 0)
         nc.vector.memset(ones[:], 1.0)
         nc.vector.memset(eps[:], EPS)
@@ -83,8 +85,6 @@ def tile_disentangledattention_pc_kernel(
             nc.sync.dma_start(out=resid_sb[:], in_=resid_rows[P * i : P * (i + 1), :])
             resid_tiles.append(resid_sb)
 
-        for j, vec in enumerate((b_f, ln2_g, ln2_b)):
-            nc.gpsimd.dma_start(out=vec_rows[0:1, j, :], in_=vec.unsqueeze(0))
         load_ff(0)
         scale_rows = Wf_scales.bitcast(I32).rearrange("g (q r) n -> r q g n", r=4)
         planes_i32 = w_planes[:].bitcast(I32)
@@ -129,8 +129,8 @@ def tile_disentangledattention_pc_kernel(
                         nc.tensor.transpose(flipped[:, gg, u, :], words, ident[:])
                 flipped_tiles[(i, bank)] = flipped
 
-        def regroup(i):
-            for bank in range(FLIP_BANKS):
+        def regroup(i, banks):
+            for bank in banks:
                 flipped = flipped_tiles[(i, bank)]
                 grouped = grouped_pool.tile([P, PASSES_PER_BANK, P, 4], BF16, align_bytes=64)
                 nc.scalar.copy(
@@ -182,7 +182,7 @@ def tile_disentangledattention_pc_kernel(
             nc.sync.dma_start(out=out_rows[P * i : P * (i + 1), :], in_=y[:])
 
         transpose(0)
-        regroup(0)
+        regroup(0, range(FLIP_BANKS))
         quantise(0)
         bias = consts.tile([P, N], BF16)
         gain = spread_pool.tile([P, N], BF16)
@@ -194,7 +194,7 @@ def tile_disentangledattention_pc_kernel(
         for i in range(ROW_BUFS):
             add_bias(i)
         transpose(1)
-        regroup(1)
+        regroup(1, range(FLIP_BANKS))
         next_accs = multiply(0)
         for cols in halves:
             nc.tensor.matmul(gain[:, cols], lhsT=ones[:], rhs=vec_rows[:, 1, cols], start=True, stop=True)
@@ -206,6 +206,8 @@ def tile_disentangledattention_pc_kernel(
             u = rows_pool.tile([P, N], F32)
             sums = stats.tile([P, HALVES], F32)
             negmean = stats.tile([P, 1], F32)
+            if i + 1 < TOKEN_TILES:
+                quantise(i + 1)
             for h in range(HALVES):
                 nc.vector.scalar_tensor_tensor(
                     out=u[:, halves[h]],
@@ -216,19 +218,22 @@ def tile_disentangledattention_pc_kernel(
                     op1=ALU.add,
                     accum_out=sums[:, h : h + 1],
                 )
-                if h == 0 and i + 1 < TOKEN_TILES:
-                    quantise(i + 1)
-            scaled = stats.tile([P, HALVES], F32)
-            nc.scalar.activation(
-                out=scaled[:], in_=sums[:], func=ACT.Copy, scale=-1.0 / N, accum_out=negmean[:]
-            )
-            if i > 0:
-                finish(i - 1)
 
             if i + AHEAD < TOKEN_TILES:
                 transpose(i + AHEAD)
             if i + 1 < TOKEN_TILES:
                 next_accs = multiply(i + 1)
+
+            if i + AHEAD < TOKEN_TILES:
+                regroup(i + AHEAD, range(1))
+            scaled = stats.tile([P, HALVES], F32)
+            nc.scalar.activation(
+                out=scaled[:], in_=sums[:], func=ACT.Copy, scale=-1.0 / N, accum_out=negmean[:]
+            )
+            if i + AHEAD < TOKEN_TILES:
+                regroup(i + AHEAD, range(1, FLIP_BANKS))
+            if i > 0:
+                finish(i - 1)
 
             squares = rows_pool.tile([P, N], BF16)
             sumsq = stats.tile([P, 1], F32)
@@ -239,8 +244,6 @@ def tile_disentangledattention_pc_kernel(
             nc.scalar.activation(
                 out=rstd[:], in_=sumsq[:], func=ACT.Abs_reciprocal_sqrt, bias=eps[:], scale=1.0 / N
             )
-            if i + AHEAD < TOKEN_TILES:
-                regroup(i + AHEAD)
             if FIRST_SORTED <= i + SORT_AHEAD < TOKEN_TILES:
                 sort_words(i + SORT_AHEAD)
 

@@ -28,6 +28,8 @@ PASSES_PER_BANK = 2
 FLIP_BANKS = PASSES // PASSES_PER_BANK
 AHEAD = 2
 ROW_BUFS = 3
+FIRST_BESIDE = 5
+LAST_PIECES = 2
 FIRST_SORTED = 4
 SORT_AHEAD = 4
 
@@ -174,12 +176,21 @@ def tile_disentangledattention_pc_kernel(
                 )
             biased_tiles[i] = biased
 
-        def finish(i):
+        def finish(i, pieces):
             y, rstd = unfinished[i]
-            nc.vector.scalar_tensor_tensor(
-                out=y[:], in0=y[:], scalar=rstd[:], in1=shift[:], op0=ALU.mult, op1=ALU.add
-            )
-            nc.sync.dma_start(out=out_rows[P * i : P * (i + 1), :], in_=y[:])
+            for c in range(pieces):
+                cols = slice(N // pieces * c, N // pieces * (c + 1))
+                nc.vector.scalar_tensor_tensor(
+                    out=y[:, cols], in0=y[:, cols], scalar=rstd[:], in1=shift[:, cols], op0=ALU.mult, op1=ALU.add
+                )
+                nc.sync.dma_start(out=out_rows[P * i : P * (i + 1), cols], in_=y[:, cols])
+
+        def finish_beside(i):
+            y, rstd = unfinished[i]
+            for cols in halves:
+                nc.scalar.activation(out=y[:, cols], in_=y[:, cols], func=ACT.Copy, scale=rstd[:])
+                nc.gpsimd.tensor_tensor(out=y[:, cols], in0=y[:, cols], in1=shift_sb[:, cols], op=ALU.add)
+                nc.sync.dma_start(out=out_rows[P * i : P * (i + 1), cols], in_=y[:, cols])
 
         transpose(0)
         regroup(0, range(FLIP_BANKS))
@@ -199,6 +210,8 @@ def tile_disentangledattention_pc_kernel(
         for cols in halves:
             nc.tensor.matmul(gain[:, cols], lhsT=ones[:], rhs=vec_rows[:, 1, cols], start=True, stop=True)
             nc.tensor.matmul(shift[:, cols], lhsT=ones[:], rhs=vec_rows[:, 2, cols], start=True, stop=True)
+        shift_sb = consts.tile([P, N], BF16)
+        nc.scalar.copy(out=shift_sb[:], in_=shift[:])
 
         unfinished = {}
         for i in range(TOKEN_TILES):
@@ -208,6 +221,8 @@ def tile_disentangledattention_pc_kernel(
             negmean = stats.tile([P, 1], F32)
             if i + 1 < TOKEN_TILES:
                 quantise(i + 1)
+            if i > FIRST_BESIDE:
+                finish_beside(i - 1)
             for h in range(HALVES):
                 nc.vector.scalar_tensor_tensor(
                     out=u[:, halves[h]],
@@ -232,8 +247,8 @@ def tile_disentangledattention_pc_kernel(
             )
             if i + AHEAD < TOKEN_TILES:
                 regroup(i + AHEAD, range(1, FLIP_BANKS))
-            if i > 0:
-                finish(i - 1)
+            if 0 < i <= FIRST_BESIDE:
+                finish(i - 1, 1)
 
             squares = rows_pool.tile([P, N], BF16)
             sumsq = stats.tile([P, 1], F32)
@@ -255,4 +270,4 @@ def tile_disentangledattention_pc_kernel(
 
             if i + ROW_BUFS < TOKEN_TILES:
                 add_bias(i + ROW_BUFS)
-        finish(TOKEN_TILES - 1)
+        finish(TOKEN_TILES - 1, LAST_PIECES)

@@ -206,10 +206,10 @@ def tile_disentangledattention_pc_kernel(
             add_bias(i)
         transpose(1)
         regroup(1, range(FLIP_BANKS))
-        next_accs = multiply(0)
         for cols in halves:
             nc.tensor.matmul(gain[:, cols], lhsT=ones[:], rhs=vec_rows[:, 1, cols], start=True, stop=True)
             nc.tensor.matmul(shift[:, cols], lhsT=ones[:], rhs=vec_rows[:, 2, cols], start=True, stop=True)
+        next_accs = multiply(0)
         shift_sb = consts.tile([P, N], BF16)
         nc.scalar.copy(out=shift_sb[:], in_=shift[:])
 

@@ -65,14 +65,14 @@ def tile_disentangledattention_pc_kernel(
         ident = consts.tile([P, P], F32)
         eps = consts.tile([P, 1], F32)
         warm = consts.tile([P, 1], F32)
+        nc.vector.memset(eps[:], EPS)
+        nc.scalar.activation(out=warm[:], in_=eps[:], func=ACT.Abs_reciprocal_sqrt)
+        nc.vector.memset(w_planes[:].bitcast(I32), 0)
         nc.vector.memset(vec_rows[:].bitcast(I32), 0)
         for j, vec in enumerate((b_f, ln2_g, ln2_b)):
             nc.scalar.dma_start(out=vec_rows[0:1, j, :], in_=vec.unsqueeze(0))
-        nc.vector.memset(w_planes[:].bitcast(I32), 0)
         nc.vector.memset(ones[:], 1.0)
-        nc.vector.memset(eps[:], EPS)
         make_identity(nc, ident[:])
-        nc.scalar.activation(out=warm[:], in_=eps[:], func=ACT.Abs_reciprocal_sqrt)
 
         ff_tiles = []
         resid_tiles = []

@@ -60,19 +60,19 @@ def tile_disentangledattention_pc_kernel(
 
         w_words = consts.tile([P, PASSES, 2 * N], U8, align_bytes=64)
         w_planes = consts.tile([P, PASSES, N], U8, align_bytes=64)
-        vec_rows = consts.tile([P, 3, N], BF16)
-        ones = consts.tile([P, P], BF16)
+        vec_rows = consts.tile([P, N], BF16)
+        pick = consts.tile([P, 3], BF16)
         ident = consts.tile([P, P], F32)
         eps = consts.tile([P, 1], F32)
         warm = consts.tile([P, 1], F32)
+        nc.vector.memset(vec_rows[:].bitcast(I32), 0)
         nc.vector.memset(eps[:], EPS)
+        for j, vec in enumerate((b_f, ln2_g, ln2_b)):
+            nc.scalar.dma_start(out=vec_rows[j : j + 1, :], in_=vec.unsqueeze(0))
         nc.scalar.activation(out=warm[:], in_=eps[:], func=ACT.Abs_reciprocal_sqrt)
         nc.vector.memset(w_planes[:].bitcast(I32), 0)
-        nc.vector.memset(vec_rows[:].bitcast(I32), 0)
-        for j, vec in enumerate((b_f, ln2_g, ln2_b)):
-            nc.scalar.dma_start(out=vec_rows[0:1, j, :], in_=vec.unsqueeze(0))
-        nc.vector.memset(ones[:], 1.0)
         make_identity(nc, ident[:])
+        nc.vector.tensor_copy(out=pick[:], in_=ident[:, 0:3])
 
         ff_tiles = []
         resid_tiles = []
@@ -192,6 +192,9 @@ def tile_disentangledattention_pc_kernel(
                 nc.gpsimd.tensor_tensor(out=y[:, cols], in0=y[:, cols], in1=shift_sb[:, cols], op=ALU.add)
                 nc.sync.dma_start(out=out_rows[P * i : P * (i + 1), cols], in_=y[:, cols])
 
+        def spread(j):
+            return pick[:, j : j + 1].to_broadcast([P, P])
+
         transpose(0)
         regroup(0, range(FLIP_BANKS))
         quantise(0)
@@ -200,15 +203,15 @@ def tile_disentangledattention_pc_kernel(
         shift = spread_pool.tile([P, N], BF16)
         for cols in halves:
             acc = acc_pool.tile([P, BANK], F32, name="acc")
-            nc.tensor.matmul(acc[:], lhsT=ones[:], rhs=vec_rows[:, 0, cols], start=True, stop=True)
+            nc.tensor.matmul(acc[:], lhsT=spread(0), rhs=vec_rows[:, cols], start=True, stop=True)
             nc.vector.tensor_copy(out=bias[:, cols], in_=acc[:])
         for i in range(ROW_BUFS):
             add_bias(i)
         transpose(1)
         regroup(1, range(FLIP_BANKS))
         for cols in halves:
-            nc.tensor.matmul(gain[:, cols], lhsT=ones[:], rhs=vec_rows[:, 1, cols], start=True, stop=True)
-            nc.tensor.matmul(shift[:, cols], lhsT=ones[:], rhs=vec_rows[:, 2, cols], start=True, stop=True)
+            nc.tensor.matmul(gain[:, cols], lhsT=spread(1), rhs=vec_rows[:, cols], start=True, stop=True)
+            nc.tensor.matmul(shift[:, cols], lhsT=spread(2), rhs=vec_rows[:, cols], start=True, stop=True)
         next_accs = multiply(0)
         shift_sb = consts.tile([P, N], BF16)
         nc.scalar.copy(out=shift_sb[:], in_=shift[:])

@@ -26,6 +26,7 @@ BANK = 512
 HALVES = N // BANK
 PASSES_PER_BANK = 2
 FLIP_BANKS = PASSES // PASSES_PER_BANK
+PASSES_PER_LOAD = 2
 AHEAD = 2
 ROW_BUFS = 3
 FIRST_BESIDE = 5
@@ -43,6 +44,8 @@ def tile_disentangledattention_pc_kernel(
     ff_rows = ff.rearrange("b s k -> (b s) k")
     resid_rows = attn_out.rearrange("b s n -> (b s) n")
     out_rows = out.rearrange("b s n -> (b s) n")
+    by_half = [(h, g) for h in range(HALVES) for g in range(PASSES)]
+    by_pass = [(h, g) for g in range(PASSES) for h in range(HALVES)]
     halves = [slice(BANK * h, BANK * (h + 1)) for h in range(HALVES)]
 
     with ExitStack() as ctx:
@@ -93,12 +96,12 @@ def tile_disentangledattention_pc_kernel(
         for r in range(4):
             nc.sync.dma_start(out=planes_i32[r : P : 32], in_=scale_rows[r])
         load_ff(1)
+        word_rows = Wf_words.bitcast(I32).rearrange("g p c -> p g c")
+        words_i32 = w_words[:].bitcast(I32)
+        for g in range(0, PASSES, PASSES_PER_LOAD):
+            some = slice(g, g + PASSES_PER_LOAD)
+            nc.sync.dma_start(out=words_i32[:, some, :], in_=word_rows[:, some, :])
         load_resid(0)
-        word_rows = Wf_words.bitcast(I32).rearrange("g p (h c) -> h p g c", h=HALVES)
-        words_i32 = w_words[:].bitcast(I32).rearrange("p g (h c) -> h p g c", h=HALVES)
-        for h in range(HALVES):
-            for g in range(0, PASSES, 3):
-                nc.sync.dma_start(out=words_i32[h][:, g : g + 3, :], in_=word_rows[h][:, g : g + 3, :])
         for i in range(AHEAD, TOKEN_TILES + 1):
             if i < TOKEN_TILES:
                 load_ff(i)
@@ -152,20 +155,19 @@ def tile_disentangledattention_pc_kernel(
                 )
             code_tiles[i] = (codes, planes)
 
-        def multiply(i):
+        def multiply(i, order):
             codes, planes = code_tiles[i]
             accs = [acc_pool.tile([P, BANK], F32, name="acc") for h in range(HALVES)]
-            for h in range(HALVES):
-                for g in range(PASSES):
-                    nc.tensor.matmul_mx(
-                        out=accs[h][:],
-                        lhsT=codes[:, g, :].bitcast(FP8X4),
-                        lhsT_scale=planes[:, g, :],
-                        rhs=w_words[:, g, 2 * BANK * h : 2 * BANK * (h + 1)].bitcast(FP4X4),
-                        rhs_scale=w_planes[:, g, halves[h]],
-                        start=(g == 0),
-                        stop=(g == PASSES - 1),
-                    )
+            for h, g in order:
+                nc.tensor.matmul_mx(
+                    out=accs[h][:],
+                    lhsT=codes[:, g, :].bitcast(FP8X4),
+                    lhsT_scale=planes[:, g, :],
+                    rhs=w_words[:, g, 2 * BANK * h : 2 * BANK * (h + 1)].bitcast(FP4X4),
+                    rhs_scale=w_planes[:, g, halves[h]],
+                    start=(g == 0),
+                    stop=(g == PASSES - 1),
+                )
             return accs
 
         def add_bias(i):
@@ -212,7 +214,7 @@ def tile_disentangledattention_pc_kernel(
         for cols in halves:
             nc.tensor.matmul(gain[:, cols], lhsT=spread(1), rhs=vec_rows[:, cols], start=True, stop=True)
             nc.tensor.matmul(shift[:, cols], lhsT=spread(2), rhs=vec_rows[:, cols], start=True, stop=True)
-        next_accs = multiply(0)
+        next_accs = multiply(0, by_pass)
         shift_sb = consts.tile([P, N], BF16)
         nc.scalar.copy(out=shift_sb[:], in_=shift[:])
 
@@ -240,7 +242,7 @@ def tile_disentangledattention_pc_kernel(
             if i + AHEAD < TOKEN_TILES:
                 transpose(i + AHEAD)
             if i + 1 < TOKEN_TILES:
-                next_accs = multiply(i + 1)
+                next_accs = multiply(i + 1, by_half)
 
             if i + AHEAD < TOKEN_TILES:
                 regroup(i + AHEAD, range(1))

@@ -32,6 +32,7 @@ ROW_BUFS = 3
 FIRST_BESIDE = 5
 LAST_PIECES = 2
 FIRST_SORTED = 4
+SORTED_PASSES = 3
 SORT_AHEAD = 4
 
 FLOPS = 2 * TOKENS * K * N
@@ -116,8 +117,13 @@ def tile_disentangledattention_pc_kernel(
 
         def sort_words(i):
             pairs = ff_tiles[i][:].bitcast(F32)
-            in_order = sorted_pool.tile([P, PASSES, 2, P], F32)
-            nc.scalar.copy(out=in_order[:], in_=pairs.rearrange("t (g p u) -> t g u p", g=PASSES, u=2))
+            in_order = sorted_pool.tile([P, SORTED_PASSES, 2, P], F32)
+            nc.scalar.copy(
+                out=in_order[:],
+                in_=pairs[:, : SORTED_PASSES * PAIRS_PER_PASS].rearrange(
+                    "t (g p u) -> t g u p", g=SORTED_PASSES, u=2
+                ),
+            )
             sorted_tiles[i] = in_order
 
         def transpose(i):
@@ -125,10 +131,11 @@ def tile_disentangledattention_pc_kernel(
             for bank in range(FLIP_BANKS):
                 flipped = flipped_pool.tile([P, PASSES_PER_BANK, 2, P], F32)
                 for gg in range(PASSES_PER_BANK):
-                    first = PAIRS_PER_PASS * (PASSES_PER_BANK * bank + gg)
+                    g = PASSES_PER_BANK * bank + gg
+                    first = PAIRS_PER_PASS * g
                     for u in range(2):
-                        if i in sorted_tiles:
-                            words = sorted_tiles[i][:, PASSES_PER_BANK * bank + gg, u, :]
+                        if i in sorted_tiles and g < SORTED_PASSES:
+                            words = sorted_tiles[i][:, g, u, :]
                         else:
                             words = pairs[:, first + u : first + PAIRS_PER_PASS : 2]
                         nc.tensor.transpose(flipped[:, gg, u, :], words, ident[:])

@@ -27,6 +27,7 @@ HALVES = N // BANK
 PASSES_PER_BANK = 2
 FLIP_BANKS = PASSES // PASSES_PER_BANK
 PASSES_PER_LOAD = 2
+EARLY = 3
 AHEAD = 2
 ROW_BUFS = 3
 FIRST_BESIDE = 5
@@ -54,7 +55,7 @@ def tile_disentangledattention_pc_kernel(
         inputs = ctx.enter_context(tc.tile_pool(name="inputs", bufs=TOKEN_TILES))
         sorted_pool = ctx.enter_context(tc.tile_pool(name="sorted", bufs=3))
         grouped_pool = ctx.enter_context(tc.tile_pool(name="grouped", bufs=2 * FLIP_BANKS))
-        codes_pool = ctx.enter_context(tc.tile_pool(name="codes", bufs=2))
+        codes_pool = ctx.enter_context(tc.tile_pool(name="codes", bufs=EARLY))
         rows_pool = ctx.enter_context(tc.tile_pool(name="rows", bufs=ROW_BUFS))
         stats = ctx.enter_context(tc.tile_pool(name="stats", bufs=ROW_BUFS))
         spread_pool = ctx.enter_context(tc.psum_pool(name="spread", bufs=1))
@@ -99,14 +100,16 @@ def tile_disentangledattention_pc_kernel(
         load_ff(1)
         word_rows = Wf_words.bitcast(I32).rearrange("g p c -> p g c")
         words_i32 = w_words[:].bitcast(I32)
+        load_ff(2)
         for g in range(0, PASSES, PASSES_PER_LOAD):
             some = slice(g, g + PASSES_PER_LOAD)
             nc.sync.dma_start(out=words_i32[:, some, :], in_=word_rows[:, some, :])
-        load_resid(0)
-        for i in range(AHEAD, TOKEN_TILES + 1):
+            if g == 0:
+                load_resid(0)
+        for i in range(EARLY, TOKEN_TILES + 2):
             if i < TOKEN_TILES:
                 load_ff(i)
-            load_resid(i - 1)
+            load_resid(i - 2)
 
         flipped_tiles = {}
         grouped_tiles = {}
@@ -216,11 +219,12 @@ def tile_disentangledattention_pc_kernel(
             nc.vector.tensor_copy(out=bias[:, cols], in_=acc[:])
         for i in range(ROW_BUFS):
             add_bias(i)
-        transpose(1)
-        regroup(1, range(FLIP_BANKS))
-        for cols in halves:
-            nc.tensor.matmul(gain[:, cols], lhsT=spread(1), rhs=vec_rows[:, cols], start=True, stop=True)
-            nc.tensor.matmul(shift[:, cols], lhsT=spread(2), rhs=vec_rows[:, cols], start=True, stop=True)
+        for i, row in zip(range(1, EARLY), (gain, shift)):
+            for cols in halves:
+                nc.tensor.matmul(row[:, cols], lhsT=spread(i), rhs=vec_rows[:, cols], start=True, stop=True)
+            transpose(i)
+            regroup(i, range(FLIP_BANKS))
+            quantise(i)
         next_accs = multiply(0, by_pass)
         shift_sb = consts.tile([P, N], BF16)
         nc.scalar.copy(out=shift_sb[:], in_=shift[:])
@@ -231,7 +235,7 @@ def tile_disentangledattention_pc_kernel(
             u = rows_pool.tile([P, N], F32)
             sums = stats.tile([P, HALVES], F32)
             negmean = stats.tile([P, 1], F32)
-            if i + 1 < TOKEN_TILES:
+            if EARLY <= i + 1 < TOKEN_TILES:
                 quantise(i + 1)
             if i > FIRST_BESIDE:
                 finish_beside(i - 1)
@@ -246,18 +250,18 @@ def tile_disentangledattention_pc_kernel(
                     accum_out=sums[:, h : h + 1],
                 )
 
-            if i + AHEAD < TOKEN_TILES:
+            if EARLY <= i + AHEAD < TOKEN_TILES:
                 transpose(i + AHEAD)
             if i + 1 < TOKEN_TILES:
                 next_accs = multiply(i + 1, by_half)
 
-            if i + AHEAD < TOKEN_TILES:
+            if EARLY <= i + AHEAD < TOKEN_TILES:
                 regroup(i + AHEAD, range(1))
             scaled = stats.tile([P, HALVES], F32)
             nc.scalar.activation(
                 out=scaled[:], in_=sums[:], func=ACT.Copy, scale=-1.0 / N, accum_out=negmean[:]
             )
-            if i + AHEAD < TOKEN_TILES:
+            if EARLY <= i + AHEAD < TOKEN_TILES:
                 regroup(i + AHEAD, range(1, FLIP_BANKS))
             if 0 < i <= FIRST_BESIDE:
                 finish(i - 1, 1)

from contextlib import ExitStack

import concourse.mybir as mybir
from concourse.masks import make_identity

F32 = mybir.dt.float32
BF16 = mybir.dt.bfloat16
I32 = mybir.dt.int32
U8 = mybir.dt.uint8
U32 = mybir.dt.uint32
FP8X4 = mybir.dt.float8_e4m3fn_x4
FP4X4 = mybir.dt.float4_e2m1fn_x4
ALU = mybir.AluOpType
ACT = mybir.ActivationFunctionType

P = 128
TOKENS = 1024
K = 3072
N = 1024
EPS = 1e-7
K_PASS = 4 * P
PASSES = K // K_PASS
PAIRS_PER_PASS = K_PASS // 2
TOKEN_TILES = TOKENS // P
BANK = 512
HALVES = N // BANK
PASSES_PER_BANK = 2
FLIP_BANKS = PASSES // PASSES_PER_BANK
PASSES_PER_LOAD = 2
EARLY = 3
AHEAD = 2
ROW_BUFS = 3
FIRST_BESIDE = 5
LAST_PIECES = 2
FIRST_SORTED = 4
SORTED_PASSES = 3
SORT_AHEAD = 4

FLOPS = 2 * TOKENS * K * N


def tile_disentangledattention_pc_kernel(
    tc, ff, attn_out, Wf_words, Wf_scales, b_f, ln2_g, ln2_b, out
):
    nc = tc.nc
    ff_rows = ff.rearrange("b s k -> (b s) k")
    resid_rows = attn_out.rearrange("b s n -> (b s) n")
    out_rows = out.rearrange("b s n -> (b s) n")
    by_half = [(h, g) for h in range(HALVES) for g in range(PASSES)]
    by_pass = [(h, g) for g in range(PASSES) for h in range(HALVES)]
    halves = [slice(BANK * h, BANK * (h + 1)) for h in range(HALVES)]

    with ExitStack() as ctx:
        consts = ctx.enter_context(tc.tile_pool(name="consts", bufs=1))
        inputs = ctx.enter_context(tc.tile_pool(name="inputs", bufs=TOKEN_TILES))
        sorted_pool = ctx.enter_context(tc.tile_pool(name="sorted", bufs=3))
        grouped_pool = ctx.enter_context(tc.tile_pool(name="grouped", bufs=2 * FLIP_BANKS))
        codes_pool = ctx.enter_context(tc.tile_pool(name="codes", bufs=EARLY))
        rows_pool = ctx.enter_context(tc.tile_pool(name="rows", bufs=ROW_BUFS))
        stats = ctx.enter_context(tc.tile_pool(name="stats", bufs=ROW_BUFS))
        spread_pool = ctx.enter_context(tc.psum_pool(name="spread", bufs=1))
        flipped_pool = ctx.enter_context(tc.psum_pool(name="flipped", bufs=FLIP_BANKS))
        acc_pool = ctx.enter_context(tc.psum_pool(name="acc", bufs=3))
        ctx.enter_context(tc.manual_schedule())

        w_words = consts.tile([P, PASSES, 2 * N], U8, align_bytes=64)
        w_planes = consts.tile([P, PASSES, N], U8, align_bytes=64)
        vec_rows = consts.tile([P, N], BF16)
        pick = consts.tile([P, 3], BF16)
        ident = consts.tile([P, P], F32)
        eps = consts.tile([P, 1], F32)
        warm = consts.tile([P, 1], F32)
        nc.vector.memset(vec_rows[:].bitcast(I32), 0)
        nc.vector.memset(eps[:], EPS)
        for j, vec in enumerate((b_f, ln2_g, ln2_b)):
            nc.scalar.dma_start(out=vec_rows[j : j + 1, :], in_=vec.unsqueeze(0))
        nc.scalar.activation(out=warm[:], in_=eps[:], func=ACT.Abs_reciprocal_sqrt)
        nc.vector.memset(w_planes[:].bitcast(I32), 0)
        make_identity(nc, ident[:])
        nc.vector.tensor_copy(out=pick[:], in_=ident[:, 0:3])

        ff_tiles = []
        resid_tiles = []

        def load_ff(i):
            ff_sb = inputs.tile([P, K], BF16)
            nc.sync.dma_start(out=ff_sb[:], in_=ff_rows[P * i : P * (i + 1), :])
            ff_tiles.append(ff_sb)

        def load_resid(i):
            resid_sb = inputs.tile([P, N], BF16)
            nc.sync.dma_start(out=resid_sb[:], in_=resid_rows[P * i : P * (i + 1), :])
            resid_tiles.append(resid_sb)

        load_ff(0)
        scale_rows = Wf_scales.bitcast(I32).rearrange("g (q r) n -> r q g n", r=4)
        planes_i32 = w_planes[:].bitcast(I32)
        for r in range(4):
            nc.sync.dma_start(out=planes_i32[r : P : 32], in_=scale_rows[r])
        load_ff(1)
        word_rows = Wf_words.bitcast(I32).rearrange("g p c -> p g c")
        words_i32 = w_words[:].bitcast(I32)
        load_ff(2)
        for g in range(0, PASSES, PASSES_PER_LOAD):
            some = slice(g, g + PASSES_PER_LOAD)
            nc.sync.dma_start(out=words_i32[:, some, :], in_=word_rows[:, some, :])
            if g == 0:
                load_resid(0)
        for i in range(EARLY, TOKEN_TILES + 2):
            if i < TOKEN_TILES:
                load_ff(i)
            load_resid(i - 2)

        flipped_tiles = {}
        grouped_tiles = {}
        code_tiles = {}
        biased_tiles = {}

        sorted_tiles = {}

        def sort_words(i):
            pairs = ff_tiles[i][:].bitcast(F32)
            in_order = sorted_pool.tile([P, SORTED_PASSES, 2, P], F32)
            nc.scalar.copy(
                out=in_order[:],
                in_=pairs[:, : SORTED_PASSES * PAIRS_PER_PASS].rearrange(
                    "t (g p u) -> t g u p", g=SORTED_PASSES, u=2
                ),
            )
            sorted_tiles[i] = in_order

        def transpose(i):
            pairs = ff_tiles[i][:].bitcast(F32)
            for bank in range(FLIP_BANKS):
                flipped = flipped_pool.tile([P, PASSES_PER_BANK, 2, P], F32)
                for gg in range(PASSES_PER_BANK):
                    g = PASSES_PER_BANK * bank + gg
                    first = PAIRS_PER_PASS * g
                    for u in range(2):
                        if i in sorted_tiles and g < SORTED_PASSES:
                            words = sorted_tiles[i][:, g, u, :]
                        else:
                            words = pairs[:, first + u : first + PAIRS_PER_PASS : 2]
                        nc.tensor.transpose(flipped[:, gg, u, :], words, ident[:])
                flipped_tiles[(i, bank)] = flipped

        def regroup(i, banks):
            for bank in banks:
                flipped = flipped_tiles[(i, bank)]
                grouped = grouped_pool.tile([P, PASSES_PER_BANK, P, 4], BF16, align_bytes=64)
                nc.scalar.copy(
                    out=grouped[:].bitcast(F32), in_=flipped[:].rearrange("p g u t -> p g t u")
                )
                grouped_tiles[(i, bank)] = grouped

        def quantise(i):
            codes = codes_pool.tile([P, PASSES, P], U32, align_bytes=64)
            planes = codes_pool.tile([P, PASSES, P], U8, align_bytes=64)
            for bank in range(FLIP_BANKS):
                some = slice(PASSES_PER_BANK * bank, PASSES_PER_BANK * (bank + 1))
                nc.vector.quantize_mx(
                    out=codes[:, some, :].rearrange("p g t -> p (g t)").bitcast(FP8X4),
                    scales=planes[:, some, :].rearrange("p g t -> p (g t)"),
                    in_=grouped_tiles[(i, bank)][:].rearrange("p g t e -> p (g t e)"),
                )
            code_tiles[i] = (codes, planes)

        def multiply(i, order):
            codes, planes = code_tiles[i]
            accs = [acc_pool.tile([P, BANK], F32, name="acc") for h in range(HALVES)]
            for h, g in order:
                nc.tensor.matmul_mx(
                    out=accs[h][:],
                    lhsT=codes[:, g, :].bitcast(FP8X4),
                    lhsT_scale=planes[:, g, :],
                    rhs=w_words[:, g, 2 * BANK * h : 2 * BANK * (h + 1)].bitcast(FP4X4),
                    rhs_scale=w_planes[:, g, halves[h]],
                    start=(g == 0),
                    stop=(g == PASSES - 1),
                )
            return accs

        def add_bias(i):
            biased = rows_pool.tile([P, N], F32)
            for cols in halves:
                nc.gpsimd.tensor_tensor(
                    out=biased[:, cols], in0=resid_tiles[i][:, cols], in1=bias[:, cols], op=ALU.add
                )
            biased_tiles[i] = biased

        def finish(i, pieces):
            y, rstd = unfinished[i]
            for c in range(pieces):
                cols = slice(N // pieces * c, N // pieces * (c + 1))
                nc.vector.scalar_tensor_tensor(
                    out=y[:, cols], in0=y[:, cols], scalar=rstd[:], in1=shift[:, cols], op0=ALU.mult, op1=ALU.add
                )
                nc.sync.dma_start(out=out_rows[P * i : P * (i + 1), cols], in_=y[:, cols])

        def finish_beside(i):
            y, rstd = unfinished[i]
            for cols in halves:
                nc.scalar.activation(out=y[:, cols], in_=y[:, cols], func=ACT.Copy, scale=rstd[:])
                nc.gpsimd.tensor_tensor(out=y[:, cols], in0=y[:, cols], in1=shift_sb[:, cols], op=ALU.add)
                nc.sync.dma_start(out=out_rows[P * i : P * (i + 1), cols], in_=y[:, cols])

        def spread(j):
            return pick[:, j : j + 1].to_broadcast([P, P])

        transpose(0)
        regroup(0, range(FLIP_BANKS))
        quantise(0)
        bias = consts.tile([P, N], BF16)
        gain = spread_pool.tile([P, N], BF16)
        shift = spread_pool.tile([P, N], BF16)
        for cols in halves:
            acc = acc_pool.tile([P, BANK], F32, name="acc")
            nc.tensor.matmul(acc[:], lhsT=spread(0), rhs=vec_rows[:, cols], start=True, stop=True)
            nc.vector.tensor_copy(out=bias[:, cols], in_=acc[:])
        for i in range(ROW_BUFS):
            add_bias(i)
        for i, row in zip(range(1, EARLY), (gain, shift)):
            for cols in halves:
                nc.tensor.matmul(row[:, cols], lhsT=spread(i), rhs=vec_rows[:, cols], start=True, stop=True)
            transpose(i)
            regroup(i, range(FLIP_BANKS))
            quantise(i)
        next_accs = multiply(0, by_pass)
        shift_sb = consts.tile([P, N], BF16)
        nc.scalar.copy(out=shift_sb[:], in_=shift[:])

        unfinished = {}
        for i in range(TOKEN_TILES):
            accs = next_accs
            u = rows_pool.tile([P, N], F32)
            sums = stats.tile([P, HALVES], F32)
            negmean = stats.tile([P, 1], F32)
            if EARLY <= i + 1 < TOKEN_TILES:
                quantise(i + 1)
            if i > FIRST_BESIDE:
                finish_beside(i - 1)
            for h in range(HALVES):
                nc.vector.scalar_tensor_tensor(
                    out=u[:, halves[h]],
                    in0=accs[h][:],
                    scalar=1.0,
                    in1=biased_tiles[i][:, halves[h]],
                    op0=ALU.mult,
                    op1=ALU.add,
                    accum_out=sums[:, h : h + 1],
                )

            if EARLY <= i + AHEAD < TOKEN_TILES:
                transpose(i + AHEAD)
            if i + 1 < TOKEN_TILES:
                next_accs = multiply(i + 1, by_half)

            if EARLY <= i + AHEAD < TOKEN_TILES:
                regroup(i + AHEAD, range(1))
            scaled = stats.tile([P, HALVES], F32)
            nc.scalar.activation(
                out=scaled[:], in_=sums[:], func=ACT.Copy, scale=-1.0 / N, accum_out=negmean[:]
            )
            if EARLY <= i + AHEAD < TOKEN_TILES:
                regroup(i + AHEAD, range(1, FLIP_BANKS))
            if 0 < i <= FIRST_BESIDE:
                finish(i - 1, 1)

            squares = rows_pool.tile([P, N], BF16)
            sumsq = stats.tile([P, 1], F32)
            rstd = stats.tile([P, 1], F32)
            nc.scalar.activation(
                out=squares[:], in_=u[:], func=ACT.Square, bias=negmean[:], scale=1.0, accum_out=sumsq[:]
            )
            nc.scalar.activation(
                out=rstd[:], in_=sumsq[:], func=ACT.Abs_reciprocal_sqrt, bias=eps[:], scale=1.0 / N
            )
            if FIRST_SORTED <= i + SORT_AHEAD < TOKEN_TILES:
                sort_words(i + SORT_AHEAD)

            y = rows_pool.tile([P, N], F32)
            nc.vector.scalar_tensor_tensor(
                out=y[:], in0=u[:], scalar=negmean[:], in1=gain[:], op0=ALU.add, op1=ALU.mult
            )
            unfinished[i] = (y, rstd)

            if i + ROW_BUFS < TOKEN_TILES:
                add_bias(i + ROW_BUFS)
        finish(TOKEN_TILES - 1, LAST_PIECES)
